import numpy as np
import ml_dtypes


def mxq(x, axis, fmt="e4m3"):
    dtype, down = {"e4m3": (ml_dtypes.float8_e4m3fn, 7), "e5m2": (ml_dtypes.float8_e5m2, 14)}[fmt]
    v = np.moveaxis(np.asarray(x, np.float32).astype(ml_dtypes.bfloat16).astype(np.float64), axis, -1)
    blocks = v.reshape(v.shape[:-1] + (-1, 32))
    amax = np.abs(blocks).max(-1, keepdims=True)
    byte = np.maximum(np.where(amax > 0, np.frexp(amax)[1] - 1 + 127, 0) - down, 1)
    scale = np.exp2(byte - 127.0)
    codes = (blocks / scale).astype(np.float32).astype(dtype).astype(np.float64)
    return np.moveaxis((codes * scale).reshape(v.shape), -1, axis)


WIDE = False


def mx_kscale(k):
    if not WIDE:
        return np.ones(k)
    levels = np.array([10, -10, 5, -5, 0])
    if k % 512:
        return np.exp2(np.random.permutation(np.resize(levels, k // 32))).repeat(32)
    a = np.empty((k // 512, 16))
    for p in range(k // 512):
        a[p, :8] = np.random.permutation(np.resize(levels, 8))
        for g in range(8):
            far = levels[np.abs(levels - a[p, g]) >= 10]
            a[p, g + 8] = far[np.random.randint(len(far))]
    return np.exp2(a.ravel()).repeat(32)


BF16 = ml_dtypes.bfloat16


def bf(x):
    return np.asarray(x, np.float32).astype(BF16)


def f64(x):
    return np.asarray(x).astype(np.float64)


B, T, DM, DH, L = 4, 512, 1024, 1024, 512


def sigmoid(x):
    return 1.0 / (1.0 + np.exp(-x))


def draw0():
    s, t = mx_kscale(DM), mx_kscale(DH)
    return {"q": bf(np.random.standard_normal((B, T, DM)) * s),
            "num": bf(np.random.standard_normal((B, T, DH)) * 1.9 * np.sqrt(T) * t),
            "den": bf(0.5 * T * (0.5 + np.random.random((B, T, DH)))),
            "Wq": bf(np.random.standard_normal((DH, DM)) / np.sqrt(DM) / s),
            "Wo": bf(np.random.standard_normal((DM, DH)) * 5.0 / np.sqrt(DH) / t)}


def core(q, num, den, Wq, Wo):
    Q = mxq(f64(q), 2, "e4m3") @ mxq(f64(Wq), 1, "e4m3").T
    Yt = sigmoid(Q) * f64(num) / f64(den)
    return mxq(Yt, 2, "e4m3") @ mxq(f64(Wo), 1, "e4m3").T


def e4m3fn_bytes(y):
    return np.clip(np.asarray(y, np.float64), -448.0, 448.0).astype(np.float32).astype(ml_dtypes.float8_e4m3fn).view(np.uint8)


def e4m3fn_values(b):
    return np.asarray(b, np.uint8).view(ml_dtypes.float8_e4m3fn).astype(np.float64)


def setup_inputs():
    d = draw0()
    x0 = np.asarray(d['q']).astype(np.float64)
    s = (np.max(np.abs(x0), axis=(0, 1), keepdims=True) / 448.0).astype(np.float32)
    out = {}
    for k, v in d.items():
        if k == 'q':
            out['q_bytes'] = e4m3fn_bytes(x0 / s.astype(np.float64))
            out['q_scale'] = s
        else:
            out[k] = v
    return out


def reference(q_bytes, q_scale, num, den, Wq, Wo):
    return core(e4m3fn_values(q_bytes) * q_scale.astype(np.float64), num, den, Wq, Wo)

@@ -1,0 +1,415 @@
+from contextlib import ExitStack
+
+import concourse.mybir as mybir
+from concourse.masks import make_identity
+
+F32 = mybir.dt.float32
+BF16 = mybir.dt.bfloat16
+U32 = mybir.dt.uint32
+U8 = mybir.dt.uint8
+FP8 = mybir.dt.float8_e4m3fn
+FP8X4 = mybir.dt.float8_e4m3fn_x4
+ACT = mybir.ActivationFunctionType
+ALU = mybir.AluOpType
+
+P = 128
+T, DM, DH, DO = 2048, 1024, 1024, 1024
+CH = 256
+NC = T // CH
+FLOPS = 2 * T * DM * DH + 2 * T * DH * DO
+
+
+def tile_aftfull_pb_kernel(tc, q_bytes, q_scale, num, den, Wq, Wo, out):
+    nc = tc.nc
+    with ExitStack() as ctx:
+        sb = ctx.enter_context(tc.tile_pool(name="sb", bufs=1))
+        ps = ctx.enter_context(tc.psum_pool(name="ps", bufs=1))
+
+        q_v = q_bytes.flatten_outer_dims().rearrange("(c p i) d -> c p i d", p=P, i=2)
+        num_v = num.flatten_outer_dims().rearrange("(c p i) d -> c p i d", p=P, i=2)
+        den_v = den.flatten_outer_dims().rearrange("(c p i) d -> c p i d", p=P, i=2)
+        out_v = out.flatten_outer_dims().rearrange("(c p i) d -> c p i d", p=P, i=2)
+        wq_v = Wq.rearrange("(g m t) k -> g m t k", m=P, t=4)
+        wo_v = Wo.rearrange("(j m) k -> j m k", m=P)
+
+        ident = sb.tile([P, P], F32, name="ident")
+        make_identity(nc, ident[:])
+        sc = sb.tile([P, 2, 4], F32, name="sc")
+
+        raw = {}
+        banks = {}
+        wts = {}
+        wq_c = {}
+        wo_c = {}
+        qb = {}
+        qx = {}
+        qt = {}
+        qc = {}
+        dent = {}
+        numt = {}
+        w = {}
+        rr = {}
+        s = {}
+        y = {}
+        yc = {}
+        o = {}
+
+        def load_sc():
+            nc.sync.dma_start(out=sc[:], in_=q_scale.rearrange("a b (g p t) -> p (a b g) t", p=P, t=4))
+
+        def load_w(key, src):
+            raw[key] = sb.tile([P, DM], BF16, name="wraw", tag="wraw", bufs=8)
+            nc.sync.dma_start(out=raw[key][:], in_=src)
+
+        def load_wq(G, t):
+            load_w(("q", G, t), wq_v[G][:, t, :])
+
+        def load_wo(j):
+            load_w(("o", j), wo_v[j])
+
+        def load_q(c):
+            qb[c] = sb.tile([P, 2, DM], U8, name="qb", tag="qb", bufs=4)
+            nc.sync.dma_start(out=qb[c][:], in_=q_v[c])
+
+        def load_den(c, i):
+            dent[c, i] = sb.tile([P, DH], BF16, name="dent", tag="dent", bufs=6)
+            nc.sync.dma_start(out=dent[c, i][:], in_=den_v[c][:, i, :])
+
+        def load_num(c):
+            numt[c] = sb.tile([P, 2, DH], BF16, name="numt", tag="numt", bufs=4)
+            nc.sync.dma_start(out=numt[c][:], in_=num_v[c])
+
+        def w_transpose(key):
+            words = raw[key][:].bitcast(F32)
+            bank = ps.tile([P, 2, 2, P], F32, name="bank_t", tag="bank_t", bufs=4)
+            for g in range(2):
+                for u in range(2):
+                    nc.tensor.transpose(bank[:, g, u, :], words[:, 256 * g + u : 256 * (g + 1) : 2], ident[:])
+            banks[key] = bank
+
+        def w_copy(key, dst, on_scalar):
+            copy = nc.scalar.copy if on_scalar else nc.vector.tensor_copy
+            copy(
+                out=dst.bitcast(F32),
+                in_=banks[key][:].rearrange("p g u m -> p g m u"),
+            )
+
+        def wq_transpose(G, t):
+            w_transpose(("q", G, t))
+
+        def wq_copy(G, t, on_scalar=False):
+            h = t // 2
+            if t % 2 == 0:
+                wts[G, h] = sb.tile([P, 2, 2, P, 4], BF16, name="wt", tag="wt", bufs=2, align_bytes=64)
+            w_copy(("q", G, t), wts[G, h][:, t % 2, :, :, :], on_scalar)
+
+        def wq_quant(G, h):
+            codes = sb.tile([P, 2, 2, P], U32, name=f"wqc{G}{h}", align_bytes=64)
+            scales = sb.tile([P, 2, 2, P], U8, name=f"wqs{G}{h}", align_bytes=64)
+            nc.vector.quantize_mx(
+                out=codes[:].rearrange("p a g m -> p (a g m)").bitcast(FP8X4),
+                scales=scales[:].rearrange("p a g m -> p (a g m)"),
+                in_=wts[G, h][:].rearrange("p a g m f -> p (a g m f)"),
+            )
+            wq_c[G, h] = (codes, scales)
+
+        def wo_transpose(j):
+            w_transpose(("o", j))
+
+        def wo_copy(j, on_scalar=False):
+            oh, jj = divmod(j, 4)
+            if jj == 0:
+                wts[oh] = sb.tile([P, 2, 512, 4], BF16, name="wot", tag="wot", bufs=1, align_bytes=64)
+            w_copy(("o", j), wts[oh][:, :, jj * P : (jj + 1) * P, :], on_scalar)
+
+        def wo_quant(oh):
+            codes = sb.tile([P, 2, 512], U32, name=f"woc{oh}", align_bytes=64)
+            scales = sb.tile([P, 2, 512], U8, name=f"wos{oh}", align_bytes=64)
+            for g in range(2):
+                nc.vector.quantize_mx(
+                    out=codes[:, g, :].bitcast(FP8X4),
+                    scales=scales[:, g, :],
+                    in_=wts[oh][:, g, :, :].rearrange("p o f -> p (o f)"),
+                )
+            wo_c[oh] = (codes, scales)
+
+        def cast(c, on_scalar=False):
+            qx[c] = sb.tile([P, 2, DM], BF16, name="qx", tag="qx", bufs=2)
+            copy = nc.scalar.copy if on_scalar else nc.vector.tensor_copy
+            copy(out=qx[c][:], in_=qb[c][:].bitcast(FP8))
+
+        def q_transpose(c, g):
+            words = qx[c][:].rearrange("p i k -> p (i k)").bitcast(F32)
+            bank = ps.tile([P, 2, 2, P], F32, name="bank_t", tag="bank_t", bufs=4)
+            for i in range(2):
+                s0 = 512 * i + 256 * g
+                for u in range(2):
+                    nc.tensor.transpose(bank[:, u, i, :], words[:, s0 + u : s0 + 256 : 2], ident[:])
+            banks["x", c, g] = bank
+
+        def q_scale_up(c, g):
+            if g == 0:
+                qt[c] = sb.tile([P, 2, CH, 4], BF16, name="qt", tag="qt", bufs=2, align_bytes=64)
+            nc.vector.tensor_tensor(
+                out=qt[c][:, g, :, :].rearrange("p n (u e) -> p n u e", u=2),
+                in0=banks["x", c, g][:].rearrange("p u i n -> p (u i n)").bitcast(BF16).rearrange("p (u n e) -> p n u e", u=2, e=2),
+                in1=sc[:, g, :].rearrange("p (u e) -> p u e", u=2).unsqueeze(1).to_broadcast([P, CH, 2, 2]),
+                op=ALU.mult,
+            )
+
+        def q_quant(c):
+            codes = sb.tile([P, 2, CH], U32, name="qcod", tag="qcod", bufs=3, align_bytes=64)
+            scales = sb.tile([P, 2, CH], U8, name="qscl", tag="qscl", bufs=3, align_bytes=64)
+            nc.vector.quantize_mx(
+                out=codes[:].rearrange("p g n -> p (g n)").bitcast(FP8X4),
+                scales=scales[:].rearrange("p g n -> p (g n)"),
+                in_=qt[c][:].rearrange("p g n f -> p (g n f)"),
+            )
+            qc[c] = (codes, scales)
+
+        def rsqrt(c, i):
+            w[c, i] = sb.tile([P, DH], F32, name="w", tag="w", bufs=16)
+            nc.scalar.activation(out=w[c, i][:], in_=dent[c, i][:], func=ACT.Abs_reciprocal_sqrt)
+
+        def square(c, i, on_gpsimd=False):
+            x = w[c, i][:]
+            if on_gpsimd:
+                nc.gpsimd.tensor_tensor(out=x, in0=x, in1=x, op=ALU.mult)
+            else:
+                nc.scalar.activation(out=x, in_=x, func=ACT.Square)
+
+        def ratio(c, i, on_vector=False):
+            rr[c, i] = sb.tile([P, 2, 4, P], F32, name="r", tag="r", bufs=4)
+            eng = nc.vector if on_vector else nc.gpsimd
+            eng.tensor_tensor(
+                out=rr[c, i][:],
+                in0=numt[c][:, i, :].rearrange("p (g m t) -> p g t m", g=2, t=4),
+                in1=w[c, i][:].rearrange("p (g m t) -> p g t m", g=2, t=4),
+                op=ALU.mult,
+            )
+
+        def m1(c, G, tp):
+            codes, scales = qc[c]
+            wc, ws = wq_c[G, tp]
+            bank = ps.tile([P, 2, CH], F32, name="bank_m", tag="bank_m", bufs=4)
+            for tt in range(2):
+                for g in range(2):
+                    nc.tensor.matmul_mx(
+                        out=bank[:, tt, :],
+                        lhsT=wc[:, tt, g, :].bitcast(FP8X4),
+                        lhsT_scale=ws[:, tt, g, :],
+                        rhs=codes[:, g, :].bitcast(FP8X4),
+                        rhs_scale=scales[:, g, :],
+                        start=(g == 0),
+                        stop=(g == 1),
+                    )
+            banks["m1", c, G, tp] = bank
+
+        def sig(c, G, tp):
+            if tp == 0:
+                s[c, G] = sb.tile([P, 4, CH], F32, name="s", tag="s", bufs=3)
+            nc.scalar.activation(out=s[c, G][:, 2 * tp : 2 * tp + 2, :], in_=banks["m1", c, G, tp][:], func=ACT.Sigmoid)
+
+        def r_transpose(c, G, i):
+            bank = ps.tile([P, 4, P], F32, name="bank_t", tag="bank_t", bufs=4)
+            for t in range(4):
+                nc.tensor.transpose(bank[:, t, :], rr[c, i][:, G, t, :], ident[:])
+            banks["r", c, G, i] = bank
+
+        def fin(c, G, i):
+            if i == 0:
+                y[c, G] = sb.tile([P, CH, 4], BF16, name="y", tag="y", bufs=3, align_bytes=64)
+            nc.vector.tensor_tensor(
+                out=y[c, G][:, i * P : (i + 1) * P, :],
+                in0=banks["r", c, G, i][:].rearrange("p t n -> p n t"),
+                in1=s[c, G][:, :, i * P : (i + 1) * P].rearrange("p t n -> p n t"),
+                op=ALU.mult,
+            )
+
+        def y_quant(c, G):
+            codes = sb.tile([P, CH], U32, name="ycod", tag="ycod", bufs=4, align_bytes=64)
+            scales = sb.tile([P, CH], U8, name="yscl", tag="yscl", bufs=4, align_bytes=64)
+            nc.vector.quantize_mx(out=codes[:].bitcast(FP8X4), scales=scales[:], in_=y[c, G][:].rearrange("p n t -> p (n t)"))
+            yc[c, G] = (codes, scales)
+
+        def m2(c, i, oh):
+            bank = ps.tile([P, 512], F32, name="bank_m", tag="bank_m", bufs=4)
+            for G in range(2):
+                codes, scales = yc[c, G]
+                nc.tensor.matmul_mx(
+                    out=bank[:],
+                    lhsT=codes[:, i * P : (i + 1) * P].bitcast(FP8X4),
+                    lhsT_scale=scales[:, i * P : (i + 1) * P],
+                    rhs=wo_c[oh][0][:, G, :].bitcast(FP8X4),
+                    rhs_scale=wo_c[oh][1][:, G, :],
+                    start=(G == 0),
+                    stop=(G == 1),
+                )
+            banks["m2", c, i, oh] = bank
+
+        def copy_out(c, i, oh, on_vector=False):
+            if oh == 0:
+                o[c, i] = sb.tile([P, DO], F32, name="o", tag="o", bufs=4)
+            copy = nc.vector.tensor_copy if on_vector else nc.scalar.copy
+            copy(out=o[c, i][:, 512 * oh : 512 * (oh + 1)], in_=banks["m2", c, i, oh][:])
+
+        def store(c, i):
+            nc.sync.dma_start(out=out_v[c][:, i, :], in_=o[c, i][:])
+
+        with tc.manual_schedule():
+
+            load_wq(0, 0)
+            load_den(0, 0)
+            load_q(0)
+            load_sc()
+            load_wq(0, 1)
+            load_den(0, 1)
+            load_wq(0, 2)
+            load_den(1, 0)
+            load_wq(0, 3)
+            rsqrt(0, 0)
+            load_den(1, 1)
+            load_wq(1, 0)
+            rsqrt(0, 1)
+            load_den(2, 0)
+            load_wq(1, 1)
+            rsqrt(1, 0)
+            load_den(2, 1)
+            load_wq(1, 2)
+            rsqrt(1, 1)
+            load_den(3, 0)
+            load_wq(1, 3)
+            load_q(1)
+            rsqrt(2, 0)
+            load_den(3, 1)
+            load_num(0)
+            rsqrt(2, 1)
+            load_den(4, 0)
+            load_wo(0)
+            load_wo(1)
+            rsqrt(3, 0)
+            load_den(4, 1)
+            load_wo(2)
+            rsqrt(3, 1)
+            load_den(5, 0)
+            load_wo(3)
+            rsqrt(4, 0)
+            load_den(5, 1)
+            load_num(1)
+            rsqrt(4, 1)
+            load_den(6, 0)
+            load_wo(4)
+            rsqrt(5, 0)
+            load_den(6, 1)
+            load_wo(5)
+            rsqrt(5, 1)
+            load_den(7, 0)
+            load_wo(6)
+            rsqrt(6, 0)
+            load_den(7, 1)
+            load_wo(7)
+            rsqrt(6, 1)
+            load_q(2)
+            load_num(2)
+            rsqrt(7, 0)
+            rsqrt(7, 1)
+            load_q(3)
+            load_num(3)
+            load_q(4)
+            load_q(5)
+            for c in range(2):
+                for i in range(2):
+                    square(c, i, on_gpsimd=True)
+                    ratio(c, i)
+
+            wq_transpose(0, 0)
+            wq_copy(0, 0)
+            cast(0)
+            wq_transpose(0, 1)
+            wq_copy(0, 1)
+            q_transpose(0, 0)
+            q_transpose(0, 1)
+            wq_transpose(0, 2)
+            q_scale_up(0, 0)
+            wq_quant(0, 0)
+            q_scale_up(0, 1)
+            wq_copy(0, 2)
+            wq_transpose(0, 3)
+            q_quant(0)
+            wq_copy(0, 3)
+            for t in range(4):
+                wq_transpose(1, t)
+                if t == 2:
+                    cast(1)
+                    wq_quant(0, 1)
+                wq_copy(1, t)
+            for g in range(2):
+                q_transpose(1, g)
+            wq_quant(1, 0)
+            q_scale_up(1, 0)
+            wq_quant(1, 1)
+            q_scale_up(1, 1)
+            for j in range(4):
+                wo_transpose(j)
+                if j == 2:
+                    q_quant(1)
+                    cast(2)
+                wo_copy(j)
+
+            for n in range(NC + 1):
+                if n < NC:
+                    for G in range(2):
+                        for tp in range(2):
+                            m1(n, G, tp)
+                            sig(n, G, tp)
+                if n == NC - 1:
+                    for G in range(2):
+                        for i in range(2):
+                            r_transpose(n, G, i)
+                            fin(n, G, i)
+                        y_quant(n, G)
+                if n == 0:
+                    wo_quant(0)
+                if n > 0:
+                    for i in range(2):
+                        for oh in range(2):
+                            m2(n - 1, i, oh)
+                            copy_out(n - 1, i, oh, on_vector=(n == NC and oh == 1))
+                        store(n - 1, i)
+                if 2 <= n + 1 < NC:
+                    for i in range(2):
+                        square(n + 1, i)
+                        ratio(n + 1, i)
+                if n < NC - 1:
+                    r_transpose(n, 0, 0)
+                    r_transpose(n, 0, 1)
+                    r_transpose(n, 1, 0)
+                    r_transpose(n, 1, 1)
+                    fin(n, 0, 0)
+                    fin(n, 0, 1)
+                    fin(n, 1, 0)
+                    y_quant(n, 0)
+                    fin(n, 1, 1)
+                    if n == 0:
+                        for j in range(4, 8):
+                            wo_transpose(j)
+                            wo_copy(j)
+                            if j == 4:
+                                y_quant(n, 1)
+                        wo_quant(1)
+                    if n + 2 < NC:
+                        q_transpose(n + 2, 0)
+                        q_transpose(n + 2, 1)
+                        q_scale_up(n + 2, 0)
+                        if n > 0:
+                            y_quant(n, 1)
+                        q_scale_up(n + 2, 1)
+                        if n + 3 < NC:
+                            cast(n + 3)
+                        q_quant(n + 2)
+                    else:
+                        y_quant(n, 1)
+                    if n + 4 < NC:
+                        load_num(n + 4)
+                    if n + 6 < NC:
+                        load_q(n + 6)

@@ -182,9 +182,9 @@ def tile_aftfull_pb_kernel(tc, q_bytes, q_scale, num, den, Wq, Wo, out):
             rr[c, i] = sb.tile([P, 2, 4, P], F32, name="r", tag="r", bufs=4)
             eng = nc.vector if on_vector else nc.gpsimd
             eng.tensor_tensor(
-                out=rr[c, i][:],
-                in0=numt[c][:, i, :].rearrange("p (g m t) -> p g t m", g=2, t=4),
-                in1=w[c, i][:].rearrange("p (g m t) -> p g t m", g=2, t=4),
+                out=rr[c, i][:].rearrange("p g t m -> p g m t"),
+                in0=numt[c][:, i, :].rearrange("p (g m t) -> p g m t", g=2, t=4),
+                in1=w[c, i][:].rearrange("p (g m t) -> p g m t", g=2, t=4),
                 op=ALU.mult,
             )
 
@@ -258,8 +258,8 @@ def tile_aftfull_pb_kernel(tc, q_bytes, q_scale, num, den, Wq, Wo, out):
 
         with tc.manual_schedule():
 
-            load_wq(0, 0)
             load_den(0, 0)
+            load_wq(0, 0)
             load_q(0)
             load_sc()
             load_wq(0, 1)
@@ -317,10 +317,10 @@ def tile_aftfull_pb_kernel(tc, q_bytes, q_scale, num, den, Wq, Wo, out):
             load_num(3)
             load_q(4)
             load_q(5)
-            for c in range(2):
+
+            for c in range(4):
                 for i in range(2):
                     square(c, i, on_gpsimd=True)
-                    ratio(c, i)
 
             wq_transpose(0, 0)
             wq_copy(0, 0)
@@ -349,11 +349,12 @@ def tile_aftfull_pb_kernel(tc, q_bytes, q_scale, num, den, Wq, Wo, out):
             q_scale_up(1, 0)
             wq_quant(1, 1)
             q_scale_up(1, 1)
+            ratio(0, 0, on_vector=True)
+            q_quant(1)
+            ratio(0, 1, on_vector=True)
+            cast(2)
             for j in range(4):
                 wo_transpose(j)
-                if j == 2:
-                    q_quant(1)
-                    cast(2)
                 wo_copy(j)
 
             for n in range(NC + 1):
@@ -376,10 +377,9 @@ def tile_aftfull_pb_kernel(tc, q_bytes, q_scale, num, den, Wq, Wo, out):
                             m2(n - 1, i, oh)
                             copy_out(n - 1, i, oh, on_vector=(n == NC and oh == 1))
                         store(n - 1, i)
-                if 2 <= n + 1 < NC:
+                if 4 <= n + 1 < NC:
                     for i in range(2):
                         square(n + 1, i)
-                        ratio(n + 1, i)
                 if n < NC - 1:
                     r_transpose(n, 0, 0)
                     r_transpose(n, 0, 1)
@@ -393,10 +393,12 @@ def tile_aftfull_pb_kernel(tc, q_bytes, q_scale, num, den, Wq, Wo, out):
                     if n == 0:
                         for j in range(4, 8):
                             wo_transpose(j)
-                            wo_copy(j)
+                            wo_copy(j, on_scalar=True)
                             if j == 4:
                                 y_quant(n, 1)
                         wo_quant(1)
+                    for i in range(2):
+                        ratio(n + 1, i, on_vector=True)
                     if n + 2 < NC:
                         q_transpose(n + 2, 0)
                         q_transpose(n + 2, 1)
@@ -405,7 +407,7 @@ def tile_aftfull_pb_kernel(tc, q_bytes, q_scale, num, den, Wq, Wo, out):
                             y_quant(n, 1)
                         q_scale_up(n + 2, 1)
                         if n + 3 < NC:
-                            cast(n + 3)
+                            cast(n + 3, on_scalar=True)
                         q_quant(n + 2)
                     else:
                         y_quant(n, 1)

from contextlib import ExitStack

import concourse.mybir as mybir
from concourse.masks import make_identity

F32 = mybir.dt.float32
BF16 = mybir.dt.bfloat16
U32 = mybir.dt.uint32
U8 = mybir.dt.uint8
FP8 = mybir.dt.float8_e4m3fn
FP8X4 = mybir.dt.float8_e4m3fn_x4
ACT = mybir.ActivationFunctionType
ALU = mybir.AluOpType

P = 128
T, DM, DH, DO = 2048, 1024, 1024, 1024
CH = 256
NC = T // CH
FLOPS = 2 * T * DM * DH + 2 * T * DH * DO


def tile_aftfull_pb_kernel(tc, q_bytes, q_scale, num, den, Wq, Wo, out):
    nc = tc.nc
    with ExitStack() as ctx:
        sb = ctx.enter_context(tc.tile_pool(name="sb", bufs=1))
        ps = ctx.enter_context(tc.psum_pool(name="ps", bufs=1))

        q_v = q_bytes.flatten_outer_dims().rearrange("(c p i) d -> c p i d", p=P, i=2)
        num_v = num.flatten_outer_dims().rearrange("(c p i) d -> c p i d", p=P, i=2)
        den_v = den.flatten_outer_dims().rearrange("(c p i) d -> c p i d", p=P, i=2)
        out_v = out.flatten_outer_dims().rearrange("(c p i) d -> c p i d", p=P, i=2)
        wq_v = Wq.rearrange("(g m t) k -> g m t k", m=P, t=4)
        wo_v = Wo.rearrange("(j m) k -> j m k", m=P)

        ident = sb.tile([P, P], F32, name="ident")
        make_identity(nc, ident[:])
        sc = sb.tile([P, 2, 4], F32, name="sc")

        raw = {}
        banks = {}
        wts = {}
        wq_c = {}
        wo_c = {}
        qb = {}
        qx = {}
        qt = {}
        qc = {}
        dent = {}
        numt = {}
        w = {}
        rr = {}
        s = {}
        y = {}
        yc = {}
        o = {}

        def load_sc():
            nc.sync.dma_start(out=sc[:], in_=q_scale.rearrange("a b (g p t) -> p (a b g) t", p=P, t=4))

        def load_w(key, src):
            raw[key] = sb.tile([P, DM], BF16, name="wraw", tag="wraw", bufs=8)
            nc.sync.dma_start(out=raw[key][:], in_=src)

        def load_wq(G, t):
            load_w(("q", G, t), wq_v[G][:, t, :])

        def load_wo(j):
            load_w(("o", j), wo_v[j])

        def load_q(c):
            qb[c] = sb.tile([P, 2, DM], U8, name="qb", tag="qb", bufs=4)
            nc.sync.dma_start(out=qb[c][:], in_=q_v[c])

        def load_den(c, i):
            dent[c, i] = sb.tile([P, DH], BF16, name="dent", tag="dent", bufs=6)
            nc.sync.dma_start(out=dent[c, i][:], in_=den_v[c][:, i, :])

        def load_num(c):
            numt[c] = sb.tile([P, 2, DH], BF16, name="numt", tag="numt", bufs=4)
            nc.sync.dma_start(out=numt[c][:], in_=num_v[c])

        def w_transpose(key):
            words = raw[key][:].bitcast(F32)
            bank = ps.tile([P, 2, 2, P], F32, name="bank_t", tag="bank_t", bufs=4)
            for g in range(2):
                for u in range(2):
                    nc.tensor.transpose(bank[:, g, u, :], words[:, 256 * g + u : 256 * (g + 1) : 2], ident[:])
            banks[key] = bank

        def w_copy(key, dst, on_scalar):
            copy = nc.scalar.copy if on_scalar else nc.vector.tensor_copy
            copy(
                out=dst.bitcast(F32),
                in_=banks[key][:].rearrange("p g u m -> p g m u"),
            )

        def wq_transpose(G, t):
            w_transpose(("q", G, t))

        def wq_copy(G, t, on_scalar=False):
            h = t // 2
            if t % 2 == 0:
                wts[G, h] = sb.tile([P, 2, 2, P, 4], BF16, name="wt", tag="wt", bufs=2, align_bytes=64)
            w_copy(("q", G, t), wts[G, h][:, t % 2, :, :, :], on_scalar)

        def wq_quant(G, h):
            codes = sb.tile([P, 2, 2, P], U32, name=f"wqc{G}{h}", align_bytes=64)
            scales = sb.tile([P, 2, 2, P], U8, name=f"wqs{G}{h}", align_bytes=64)
            nc.vector.quantize_mx(
                out=codes[:].rearrange("p a g m -> p (a g m)").bitcast(FP8X4),
                scales=scales[:].rearrange("p a g m -> p (a g m)"),
                in_=wts[G, h][:].rearrange("p a g m f -> p (a g m f)"),
            )
            wq_c[G, h] = (codes, scales)

        def wo_transpose(j):
            w_transpose(("o", j))

        def wo_copy(j, on_scalar=False):
            oh, jj = divmod(j, 4)
            if jj == 0:
                wts[oh] = sb.tile([P, 2, 512, 4], BF16, name="wot", tag="wot", bufs=1, align_bytes=64)
            w_copy(("o", j), wts[oh][:, :, jj * P : (jj + 1) * P, :], on_scalar)

        def wo_quant(oh):
            codes = sb.tile([P, 2, 512], U32, name=f"woc{oh}", align_bytes=64)
            scales = sb.tile([P, 2, 512], U8, name=f"wos{oh}", align_bytes=64)
            for g in range(2):
                nc.vector.quantize_mx(
                    out=codes[:, g, :].bitcast(FP8X4),
                    scales=scales[:, g, :],
                    in_=wts[oh][:, g, :, :].rearrange("p o f -> p (o f)"),
                )
            wo_c[oh] = (codes, scales)

        def cast(c, on_scalar=False):
            qx[c] = sb.tile([P, 2, DM], BF16, name="qx", tag="qx", bufs=2)
            copy = nc.scalar.copy if on_scalar else nc.vector.tensor_copy
            copy(out=qx[c][:], in_=qb[c][:].bitcast(FP8))

        def q_transpose(c, g):
            words = qx[c][:].rearrange("p i k -> p (i k)").bitcast(F32)
            bank = ps.tile([P, 2, 2, P], F32, name="bank_t", tag="bank_t", bufs=4)
            for i in range(2):
                s0 = 512 * i + 256 * g
                for u in range(2):
                    nc.tensor.transpose(bank[:, u, i, :], words[:, s0 + u : s0 + 256 : 2], ident[:])
            banks["x", c, g] = bank

        def q_scale_up(c, g):
            if g == 0:
                qt[c] = sb.tile([P, 2, CH, 4], BF16, name="qt", tag="qt", bufs=2, align_bytes=64)
            nc.vector.tensor_tensor(
                out=qt[c][:, g, :, :].rearrange("p n (u e) -> p n u e", u=2),
                in0=banks["x", c, g][:].rearrange("p u i n -> p (u i n)").bitcast(BF16).rearrange("p (u n e) -> p n u e", u=2, e=2),
                in1=sc[:, g, :].rearrange("p (u e) -> p u e", u=2).unsqueeze(1).to_broadcast([P, CH, 2, 2]),
                op=ALU.mult,
            )

        def q_quant(c):
            codes = sb.tile([P, 2, CH], U32, name="qcod", tag="qcod", bufs=3, align_bytes=64)
            scales = sb.tile([P, 2, CH], U8, name="qscl", tag="qscl", bufs=3, align_bytes=64)
            nc.vector.quantize_mx(
                out=codes[:].rearrange("p g n -> p (g n)").bitcast(FP8X4),
                scales=scales[:].rearrange("p g n -> p (g n)"),
                in_=qt[c][:].rearrange("p g n f -> p (g n f)"),
            )
            qc[c] = (codes, scales)

        def rsqrt(c, i):
            w[c, i] = sb.tile([P, DH], F32, name="w", tag="w", bufs=16)
            nc.scalar.activation(out=w[c, i][:], in_=dent[c, i][:], func=ACT.Abs_reciprocal_sqrt)

        def square(c, i, on_gpsimd=False):
            x = w[c, i][:]
            if on_gpsimd:
                nc.gpsimd.tensor_tensor(out=x, in0=x, in1=x, op=ALU.mult)
            else:
                nc.scalar.activation(out=x, in_=x, func=ACT.Square)

        def ratio(c, i, on_vector=False):
            rr[c, i] = sb.tile([P, 2, 4, P], F32, name="r", tag="r", bufs=4)
            eng = nc.vector if on_vector else nc.gpsimd
            eng.tensor_tensor(
                out=rr[c, i][:].rearrange("p g t m -> p g m t"),
                in0=numt[c][:, i, :].rearrange("p (g m t) -> p g m t", g=2, t=4),
                in1=w[c, i][:].rearrange("p (g m t) -> p g m t", g=2, t=4),
                op=ALU.mult,
            )

        def m1(c, G, tp):
            codes, scales = qc[c]
            wc, ws = wq_c[G, tp]
            bank = ps.tile([P, 2, CH], F32, name="bank_m", tag="bank_m", bufs=4)
            for tt in range(2):
                for g in range(2):
                    nc.tensor.matmul_mx(
                        out=bank[:, tt, :],
                        lhsT=wc[:, tt, g, :].bitcast(FP8X4),
                        lhsT_scale=ws[:, tt, g, :],
                        rhs=codes[:, g, :].bitcast(FP8X4),
                        rhs_scale=scales[:, g, :],
                        start=(g == 0),
                        stop=(g == 1),
                    )
            banks["m1", c, G, tp] = bank

        def sig(c, G, tp):
            if tp == 0:
                s[c, G] = sb.tile([P, 4, CH], F32, name="s", tag="s", bufs=3)
            nc.scalar.activation(out=s[c, G][:, 2 * tp : 2 * tp + 2, :], in_=banks["m1", c, G, tp][:], func=ACT.Sigmoid)

        def r_transpose(c, G, i):
            bank = ps.tile([P, 4, P], F32, name="bank_t", tag="bank_t", bufs=4)
            for t in range(4):
                nc.tensor.transpose(bank[:, t, :], rr[c, i][:, G, t, :], ident[:])
            banks["r", c, G, i] = bank

        def fin(c, G, i):
            if i == 0:
                y[c, G] = sb.tile([P, CH, 4], BF16, name="y", tag="y", bufs=3, align_bytes=64)
            nc.vector.tensor_tensor(
                out=y[c, G][:, i * P : (i + 1) * P, :],
                in0=banks["r", c, G, i][:].rearrange("p t n -> p n t"),
                in1=s[c, G][:, :, i * P : (i + 1) * P].rearrange("p t n -> p n t"),
                op=ALU.mult,
            )

        def y_quant(c, G):
            codes = sb.tile([P, CH], U32, name="ycod", tag="ycod", bufs=4, align_bytes=64)
            scales = sb.tile([P, CH], U8, name="yscl", tag="yscl", bufs=4, align_bytes=64)
            nc.vector.quantize_mx(out=codes[:].bitcast(FP8X4), scales=scales[:], in_=y[c, G][:].rearrange("p n t -> p (n t)"))
            yc[c, G] = (codes, scales)

        def m2(c, i, oh):
            bank = ps.tile([P, 512], F32, name="bank_m", tag="bank_m", bufs=4)
            for G in range(2):
                codes, scales = yc[c, G]
                nc.tensor.matmul_mx(
                    out=bank[:],
                    lhsT=codes[:, i * P : (i + 1) * P].bitcast(FP8X4),
                    lhsT_scale=scales[:, i * P : (i + 1) * P],
                    rhs=wo_c[oh][0][:, G, :].bitcast(FP8X4),
                    rhs_scale=wo_c[oh][1][:, G, :],
                    start=(G == 0),
                    stop=(G == 1),
                )
            banks["m2", c, i, oh] = bank

        def copy_out(c, i, oh, on_vector=False):
            if oh == 0:
                o[c, i] = sb.tile([P, DO], F32, name="o", tag="o", bufs=4)
            copy = nc.vector.tensor_copy if on_vector else nc.scalar.copy
            copy(out=o[c, i][:, 512 * oh : 512 * (oh + 1)], in_=banks["m2", c, i, oh][:])

        def store(c, i):
            nc.sync.dma_start(out=out_v[c][:, i, :], in_=o[c, i][:])

        with tc.manual_schedule():

            load_den(0, 0)
            load_wq(0, 0)
            load_q(0)
            load_sc()
            load_wq(0, 1)
            load_den(0, 1)
            load_wq(0, 2)
            load_den(1, 0)
            load_wq(0, 3)
            rsqrt(0, 0)
            load_den(1, 1)
            load_wq(1, 0)
            rsqrt(0, 1)
            load_den(2, 0)
            load_wq(1, 1)
            rsqrt(1, 0)
            load_den(2, 1)
            load_wq(1, 2)
            rsqrt(1, 1)
            load_den(3, 0)
            load_wq(1, 3)
            load_q(1)
            rsqrt(2, 0)
            load_den(3, 1)
            load_num(0)
            rsqrt(2, 1)
            load_den(4, 0)
            load_wo(0)
            load_wo(1)
            rsqrt(3, 0)
            load_den(4, 1)
            load_wo(2)
            rsqrt(3, 1)
            load_den(5, 0)
            load_wo(3)
            rsqrt(4, 0)
            load_den(5, 1)
            load_num(1)
            rsqrt(4, 1)
            load_den(6, 0)
            load_wo(4)
            rsqrt(5, 0)
            load_den(6, 1)
            load_wo(5)
            rsqrt(5, 1)
            load_den(7, 0)
            load_wo(6)
            rsqrt(6, 0)
            load_den(7, 1)
            load_wo(7)
            rsqrt(6, 1)
            load_q(2)
            load_num(2)
            rsqrt(7, 0)
            rsqrt(7, 1)
            load_q(3)
            load_num(3)
            load_q(4)
            load_q(5)

            for c in range(4):
                for i in range(2):
                    square(c, i, on_gpsimd=True)

            wq_transpose(0, 0)
            wq_copy(0, 0)
            cast(0)
            wq_transpose(0, 1)
            wq_copy(0, 1)
            q_transpose(0, 0)
            q_transpose(0, 1)
            wq_transpose(0, 2)
            q_scale_up(0, 0)
            wq_quant(0, 0)
            q_scale_up(0, 1)
            wq_copy(0, 2)
            wq_transpose(0, 3)
            q_quant(0)
            wq_copy(0, 3)
            for t in range(4):
                wq_transpose(1, t)
                if t == 2:
                    cast(1)
                    wq_quant(0, 1)
                wq_copy(1, t)
            for g in range(2):
                q_transpose(1, g)
            wq_quant(1, 0)
            q_scale_up(1, 0)
            wq_quant(1, 1)
            q_scale_up(1, 1)
            ratio(0, 0, on_vector=True)
            q_quant(1)
            ratio(0, 1, on_vector=True)
            cast(2)
            for j in range(4):
                wo_transpose(j)
                wo_copy(j)

            for n in range(NC + 1):
                if n < NC:
                    for G in range(2):
                        for tp in range(2):
                            m1(n, G, tp)
                            sig(n, G, tp)
                if n == NC - 1:
                    for G in range(2):
                        for i in range(2):
                            r_transpose(n, G, i)
                            fin(n, G, i)
                        y_quant(n, G)
                if n == 0:
                    wo_quant(0)
                if n > 0:
                    for i in range(2):
                        for oh in range(2):
                            m2(n - 1, i, oh)
                            copy_out(n - 1, i, oh, on_vector=(n == NC and oh == 1))
                        store(n - 1, i)
                if 4 <= n + 1 < NC:
                    for i in range(2):
                        square(n + 1, i)
                if n < NC - 1:
                    r_transpose(n, 0, 0)
                    r_transpose(n, 0, 1)
                    r_transpose(n, 1, 0)
                    r_transpose(n, 1, 1)
                    fin(n, 0, 0)
                    fin(n, 0, 1)
                    fin(n, 1, 0)
                    y_quant(n, 0)
                    fin(n, 1, 1)
                    if n == 0:
                        for j in range(4, 8):
                            wo_transpose(j)
                            wo_copy(j, on_scalar=True)
                            if j == 4:
                                y_quant(n, 1)
                        wo_quant(1)
                    for i in range(2):
                        ratio(n + 1, i, on_vector=True)
                    if n + 2 < NC:
                        q_transpose(n + 2, 0)
                        q_transpose(n + 2, 1)
                        q_scale_up(n + 2, 0)
                        if n > 0:
                            y_quant(n, 1)
                        q_scale_up(n + 2, 1)
                        if n + 3 < NC:
                            cast(n + 3, on_scalar=True)
                        q_quant(n + 2)
                    else:
                        y_quant(n, 1)
                    if n + 4 < NC:
                        load_num(n + 4)
                    if n + 6 < NC:
                        load_q(n + 6)
